import numpy as np
import ml_dtypes


def mxq(x, axis, fmt="e4m3"):
    dtype, down = {"e4m3": (ml_dtypes.float8_e4m3fn, 7), "e5m2": (ml_dtypes.float8_e5m2, 14)}[fmt]
    v = np.moveaxis(np.asarray(x, np.float32).astype(ml_dtypes.bfloat16).astype(np.float64), axis, -1)
    blocks = v.reshape(v.shape[:-1] + (-1, 32))
    amax = np.abs(blocks).max(-1, keepdims=True)
    byte = np.maximum(np.where(amax > 0, np.frexp(amax)[1] - 1 + 127, 0) - down, 1)
    scale = np.exp2(byte - 127.0)
    codes = (blocks / scale).astype(np.float32).astype(dtype).astype(np.float64)
    return np.moveaxis((codes * scale).reshape(v.shape), -1, axis)


WIDE = False


def mx_kscale(k):
    if not WIDE:
        return np.ones(k)
    levels = np.array([10, -10, 5, -5, 0])
    a = np.random.permutation(np.resize(levels, k // 512 * 4)).reshape(k // 512, 4)
    idx = np.arange(k)
    return np.exp2(a[idx // 512, idx % 128 // 32])


BF16 = ml_dtypes.bfloat16


def bf(x):
    return np.asarray(x, np.float32).astype(BF16)


def f64(x):
    return np.asarray(x).astype(np.float64)


E2M1 = np.array([0.0, 0.5, 1.0, 1.5, 2.0, 3.0, 4.0, 6.0, -0.0, -0.5, -1.0, -1.5, -2.0, -3.0, -4.0, -6.0])


def pack_weight(w, fmt):
    k, n = w.shape
    w = f64(bf(w)).reshape(k // 32, 32, n)
    amax = np.abs(w).max(1)
    if fmt == "e4m3":
        byte = np.frexp(amax)[1] - 1 + 127 - 7
    else:
        mant, ex = np.frexp(amax / 6.0)
        byte = np.where(mant > 0.5, ex, ex - 1) + 127
    byte = np.clip(np.where(amax > 0, byte, 1), 1, 254)
    scaled = (w * np.exp2(127.0 - byte)[:, None, :]).reshape(k, n).astype(np.float32)
    by_word = np.ascontiguousarray(scaled.reshape(k // 512, 128, 4, n).transpose(0, 1, 3, 2))
    if fmt == "e4m3":
        words = by_word.astype(ml_dtypes.float8_e4m3fn).view(np.uint8)
    else:
        c = by_word.astype(ml_dtypes.float4_e2m1fn).view(np.uint8) & 0xF
        words = c[..., 0::2] | (c[..., 1::2] << 4)
    return np.ascontiguousarray(words), np.ascontiguousarray(byte.astype(np.uint8).reshape(k // 512, 16, n))


def unpack_weight(words, scales, fmt):
    g, p, n, _ = words.shape
    if fmt == "e4m3":
        vals = np.ascontiguousarray(words).view(ml_dtypes.float8_e4m3fn).astype(np.float64)
    else:
        nib = np.empty((g, p, n, 4), np.uint8)
        nib[..., 0::2] = words & 0xF
        nib[..., 1::2] = words >> 4
        vals = E2M1[nib]
    vals = vals * np.repeat(np.exp2(scales.astype(np.float64) - 127.0), 8, axis=1)[..., None]
    return vals.transpose(0, 1, 3, 2).reshape(g * 512, n)


N, APP, SP, CARD, SUB, OUT = 4096, 512, 512, 16, 32, 1024
HID = CARD * SUB
FMT = "e4m3"


def setup_inputs():
    s1, s2 = mx_kscale(APP), mx_kscale(SP)
    t = mx_kscale(HID).reshape(CARD, SUB)
    appearance = bf(np.random.standard_normal((N, APP)) * s1)
    spatial = bf(np.random.standard_normal((N, SP)) * s2)
    w1 = np.random.standard_normal((CARD, APP, SUB)) / np.sqrt(APP) / s1[None, :, None] * t[:, None, :]
    b1 = bf(np.random.standard_normal((CARD, SUB)) * 0.2 * t)
    w2 = np.random.standard_normal((CARD, SP, SUB)) / np.sqrt(SP) / s2[None, :, None] * t[:, None, :]
    b2 = bf(np.random.standard_normal((CARD, SUB)) * 0.2 * t)
    W3 = bf(np.random.standard_normal((CARD, SUB, OUT)) / np.sqrt(HID) / t[:, :, None])
    b3 = bf(np.random.standard_normal((CARD, OUT)) * 0.4 / np.sqrt(CARD))
    W1_words, W1_scales = pack_weight(w1.reshape(-1, SUB), FMT)
    W2_words, W2_scales = pack_weight(w2.reshape(-1, SUB), FMT)
    return {
        "appearance": appearance,
        "spatial": spatial,
        "W1_words": W1_words,
        "W1_scales": W1_scales,
        "b1": b1,
        "W2_words": W2_words,
        "W2_scales": W2_scales,
        "b2": b2,
        "W3": W3,
        "b3": b3,
    }


def reference(appearance, spatial, W1_words, W1_scales, b1, W2_words, W2_scales, b2, W3, b3):
    w1 = unpack_weight(W1_words, W1_scales, FMT).reshape(CARD, APP, SUB).transpose(1, 0, 2).reshape(APP, HID)
    w2 = unpack_weight(W2_words, W2_scales, FMT).reshape(CARD, SP, SUB).transpose(1, 0, 2).reshape(SP, HID)
    h1 = (mxq(f64(appearance), 1, "e4m3") @ w1) + f64(b1).reshape(1, HID)
    h2 = (mxq(f64(spatial), 1, "e4m3") @ w2) + f64(b2).reshape(1, HID)
    h = np.maximum(h1 + h2, 0.0)
    out = (mxq(h, 1, "e4m3") @ mxq(f64(W3).reshape(HID, OUT), 0, "e4m3")) + f64(b3).sum(0)[None]
    return np.maximum(out, 0.0)

@@ -1,0 +1,255 @@
+import concourse.mybir as mybir
+from concourse.masks import make_identity
+from contextlib import ExitStack
+
+F32 = mybir.dt.float32
+BF16 = mybir.dt.bfloat16
+I32 = mybir.dt.int32
+U8 = mybir.dt.uint8
+FP8X4 = mybir.dt.float8_e4m3fn_x4
+ALU = mybir.AluOpType
+ACT = mybir.ActivationFunctionType
+
+P = 128
+PACK = 4
+BANK = 512
+ROWS, K_IN, HID, OUT = 4096, 512, 512, 1024
+CARD, SUB = 16, 32
+RUN = SUB // PACK
+ROUND = 512
+N_ROUNDS = ROWS // ROUND
+SLABS = ROUND // P
+WORDS = K_IN // 2
+F32_MAX = 3.4028234663852886e38
+
+FLOPS = 2 * ROWS * (K_IN * HID + K_IN * HID + HID * OUT)
+
+
+def tile_multibranchfusion_t_e_kernel(
+    tc, appearance, spatial, W1_words, W1_scales, b1, W2_words, W2_scales, b2, W3, b3, out
+):
+    nc = tc.nc
+    with ExitStack() as ctx:
+        ctx.enter_context(tc.manual_schedule())
+        const = ctx.enter_context(tc.tile_pool(name="const", bufs=1))
+        rows_in = ctx.enter_context(tc.tile_pool(name="rows_in", bufs=1))
+        work = ctx.enter_context(tc.tile_pool(name="work", bufs=2))
+        packed = ctx.enter_context(tc.tile_pool(name="packed", bufs=3))
+        rows_out = ctx.enter_context(tc.tile_pool(name="rows_out", bufs=3))
+        psum = ctx.enter_context(tc.psum_pool(name="psum", bufs=8))
+
+        identity = const.tile([P, P], F32)
+        make_identity(nc, identity[:])
+        w1_raw_scales = const.tile([P, CARD, SUB], U8)
+        w2_raw_scales = const.tile([P, CARD, SUB], U8)
+        nc.vector.memset(w1_raw_scales[:].bitcast(I32), 0)
+        nc.vector.memset(w2_raw_scales[:].bitcast(I32), 0)
+        b12_rows = const.tile([P, P], BF16)
+        nc.vector.memset(b12_rows[:], 0.0)
+        b3_rows = const.tile([P, OUT], BF16)
+        nc.vector.memset(b3_rows[:], 0.0)
+        ones = const.tile([P, P], BF16)
+        nc.vector.memset(ones[:], 1.0)
+
+        def load_rows(src, r, name):
+            rows = rows_in.tile([P, SLABS, K_IN], BF16, name="%s%d" % (name, r))
+            nc.sync.dma_start(
+                out=rows[:],
+                in_=src[ROUND * r : ROUND * (r + 1), :].rearrange("(p a) k -> p a k", a=SLABS),
+            )
+            return rows
+
+        def load_scale_rows(raw_scales, scales_dram):
+            for quadrant in range(4):
+                nc.sync.dma_start(
+                    out=raw_scales[32 * quadrant : 32 * quadrant + 4].bitcast(I32),
+                    in_=scales_dram.bitcast(I32)[:, 4 * quadrant : 4 * quadrant + 4, :].rearrange(
+                        "c q s -> q c s"
+                    ),
+                )
+
+        def load_words(words_dram, name):
+            raw_words = const.tile([P, CARD, SUB], I32, name=name)
+            nc.sync.dma_start(
+                out=raw_words[:], in_=words_dram.rearrange("c p s t -> p c (s t)").bitcast(I32)
+            )
+            return raw_words
+
+        app_rows = [None] * N_ROUNDS
+        sp_rows = [None] * N_ROUNDS
+        app_rows[0] = load_rows(appearance, 0, "app")
+        sp_rows[0] = load_rows(spatial, 0, "sp")
+        load_scale_rows(w1_raw_scales, W1_scales)
+        load_scale_rows(w2_raw_scales, W2_scales)
+        app_rows[1] = load_rows(appearance, 1, "app")
+        sp_rows[1] = load_rows(spatial, 1, "sp")
+        w1_raw_words = load_words(W1_words, "w1_raw_words")
+        w2_raw_words = load_words(W2_words, "w2_raw_words")
+        w3_raw = const.tile([P, PACK, OUT], BF16)
+        for t in range(PACK):
+            nc.sync.dma_start(out=w3_raw[:, t, :], in_=W3[:, RUN * t : RUN * (t + 1), :])
+        for r in range(2, N_ROUNDS):
+            app_rows[r] = load_rows(appearance, r, "app")
+            sp_rows[r] = load_rows(spatial, r, "sp")
+
+        nc.scalar.dma_start(out=b12_rows[0:PACK, :], in_=b1.rearrange("c (t i) -> t c i", i=RUN))
+        nc.scalar.dma_start(out=b12_rows[PACK : 2 * PACK, :], in_=b2.rearrange("c (t i) -> t c i", i=RUN))
+        nc.scalar.dma_start(out=b3_rows[0:CARD, :], in_=b3)
+
+        def side_by_side(copy, grouped, planes):
+            copy(
+                out=grouped.rearrange("p (c i) t -> p c t i", i=4),
+                in_=planes.rearrange("p t (c i) -> p c t i", i=4),
+            )
+
+        def transpose_and_quantise(rows, name):
+            grouped = work.tile([P, SLABS, P, PACK], BF16, name=name + "_grouped", align_bytes=64)
+            for pair in range(SLABS // 2):
+                flipped = psum.tile([P, 2, 2, P], F32, tag="bank")
+                for a in range(2):
+                    for u in range(2):
+                        nc.tensor.transpose(
+                            out=flipped[:, a, u, :],
+                            in_=rows[:, 2 * pair + a, :].bitcast(F32)[:, u:WORDS:2],
+                            identity=identity[:],
+                        )
+                nc.scalar.copy(
+                    out=grouped[:, 2 * pair : 2 * pair + 2, :, :].bitcast(F32),
+                    in_=flipped[:].rearrange("p a u n -> p a n u"),
+                )
+            words = packed.tile([P, ROUND], I32, name=name + "_words", align_bytes=64)
+            scales = packed.tile([P, ROUND], U8, name=name + "_scales", align_bytes=64)
+            nc.vector.quantize_mx(
+                out=words[:].bitcast(FP8X4),
+                scales=scales[:],
+                in_=grouped[:].rearrange("p a n t -> p (a n t)"),
+            )
+            return words, scales
+
+        def regroup_weight_bytes(raw_words, raw_scales, name):
+            words = const.tile([P, PACK, P], I32, name=name + "_words", align_bytes=64)
+            scales = const.tile([P, PACK, P], U8, name=name + "_scales", align_bytes=64)
+            nc.vector.tensor_copy(
+                out=words[:].rearrange("p t (c i) -> p t c i", i=RUN),
+                in_=raw_words[:].rearrange("p c (t i) -> p t c i", i=RUN),
+            )
+            nc.vector.tensor_copy(
+                out=scales[:].bitcast(I32).rearrange("p t (c w) -> p t c w", w=RUN // 4),
+                in_=raw_scales[:].bitcast(I32).rearrange("p c (t w) -> p t c w", w=RUN // 4),
+            )
+            return words, scales
+
+        def hidden_layer(x_app, x_sp):
+            h_planes = work.tile([P, PACK, ROUND], BF16)
+            for t in range(PACK):
+                acc = psum.tile([P, BANK], F32, tag="bank")
+                for weight, x, first in ((w1, x_app, True), (w2, x_sp, False)):
+                    nc.tensor.matmul_mx(
+                        out=acc[:],
+                        lhsT=weight[0][:, t, :].bitcast(FP8X4),
+                        lhsT_scale=weight[1][:, t, :],
+                        rhs=x[0][:].bitcast(FP8X4),
+                        rhs_scale=x[1][:],
+                        start=first,
+                        stop=not first,
+                    )
+                nc.scalar.activation(
+                    out=h_planes[:, t, :], in_=acc[:], func=ACT.Relu, bias=bias12[:, t : t + 1], scale=1.0
+                )
+            return h_planes
+
+        def quantise_hidden(h_planes):
+            h_grouped = work.tile([P, ROUND, PACK], BF16, align_bytes=64)
+            side_by_side(nc.scalar.copy, h_grouped[:], h_planes[:])
+            h_words = work.tile([P, ROUND], I32, align_bytes=64)
+            h_scales = work.tile([P, ROUND], U8, align_bytes=64)
+            nc.vector.quantize_mx(
+                out=h_words[:].bitcast(FP8X4),
+                scales=h_scales[:],
+                in_=h_grouped[:].rearrange("p n t -> p (n t)"),
+            )
+            return h_words, h_scales
+
+        def output_layer(h, r):
+            h_words, h_scales = h
+            result = rows_out.tile([P, SLABS, OUT], F32)
+            out_rows = out[ROUND * r : ROUND * (r + 1), :].rearrange("(p a) o -> p a o", a=SLABS)
+            for a in range(SLABS):
+                slab = slice(P * a, P * (a + 1))
+                for half in range(OUT // BANK):
+                    cols = slice(BANK * half, BANK * (half + 1))
+                    acc = psum.tile([P, BANK], F32, tag="bank")
+                    nc.tensor.matmul_mx(
+                        out=acc[:],
+                        lhsT=h_words[:, slab].bitcast(FP8X4),
+                        lhsT_scale=h_scales[:, slab],
+                        rhs=w3_words[:, cols].bitcast(FP8X4),
+                        rhs_scale=w3_scales[:, cols],
+                        start=True,
+                        stop=True,
+                    )
+                    nc.vector.tensor_tensor(out=result[:, a, cols], in0=acc[:], in1=bias3[:, cols], op=ALU.add)
+                nc.gpsimd.tensor_scalar(
+                    out=result[:, a, :],
+                    in0=result[:, a, :],
+                    scalar1=F32_MAX,
+                    scalar2=0.0,
+                    op0=ALU.min,
+                    op1=ALU.max,
+                )
+                if a % 2 == 1:
+                    nc.sync.dma_start(out=out_rows[:, a - 1 : a + 1, :], in_=result[:, a - 1 : a + 1, :])
+
+        x_app = [None] * N_ROUNDS
+        x_sp = [None] * N_ROUNDS
+
+        def prepare_round(r):
+            x_app[r] = transpose_and_quantise(app_rows[r], "app")
+            x_sp[r] = transpose_and_quantise(sp_rows[r], "sp")
+
+        b12_rows_f32 = const.tile([P, P], F32)
+        nc.vector.tensor_copy(out=b12_rows_f32[:], in_=b12_rows[:])
+
+        prepare_round(0)
+
+        b12_flipped = psum.tile([P, BANK], F32, tag="bank")
+        nc.tensor.transpose(out=b12_flipped[:, 0:P], in_=b12_rows_f32[:], identity=identity[:])
+        b12_cols = const.tile([P, 2 * PACK], F32)
+        nc.vector.tensor_copy(out=b12_cols[:], in_=b12_flipped[:, 0 : 2 * PACK])
+        bias12 = const.tile([P, PACK], F32)
+        nc.vector.tensor_tensor(
+            out=bias12[:], in0=b12_cols[:, 0:PACK], in1=b12_cols[:, PACK : 2 * PACK], op=ALU.add
+        )
+
+        prepare_round(1)
+
+        w1 = regroup_weight_bytes(w1_raw_words, w1_raw_scales, "w1")
+        w2 = regroup_weight_bytes(w2_raw_words, w2_raw_scales, "w2")
+
+        w3_grouped = const.tile([P, OUT, PACK], BF16, align_bytes=64)
+        side_by_side(nc.vector.tensor_copy, w3_grouped[:], w3_raw[:])
+        w3_words = const.tile([P, OUT], I32, align_bytes=64)
+        w3_scales = const.tile([P, OUT], U8, align_bytes=64)
+        nc.vector.quantize_mx(
+            out=w3_words[:].bitcast(FP8X4),
+            scales=w3_scales[:],
+            in_=w3_grouped[:].rearrange("p o t -> p (o t)"),
+        )
+
+        bias3 = const.tile([P, OUT], F32)
+        for half in range(OUT // BANK):
+            cols = slice(BANK * half, BANK * (half + 1))
+            acc = psum.tile([P, BANK], F32, tag="bank")
+            nc.tensor.matmul(out=acc[:], lhsT=ones[:], rhs=b3_rows[:, cols], start=True, stop=True)
+            nc.vector.tensor_copy(out=bias3[:, cols], in_=acc[:])
+
+        h = [None] * N_ROUNDS
+        for r in range(N_ROUNDS + 1):
+            if r < N_ROUNDS:
+                h_planes = hidden_layer(x_app[r], x_sp[r])
+            if r >= 1:
+                output_layer(h[r - 1], r - 1)
+            if r < N_ROUNDS:
+                h[r] = quantise_hidden(h_planes)
+            if r + 2 < N_ROUNDS:
+                prepare_round(r + 2)

@@ -21,6 +21,7 @@ N_ROUNDS = ROWS // ROUND
 SLABS = ROUND // P
 WORDS = K_IN // 2
 F32_MAX = 3.4028234663852886e38
+VECTOR_SLAB = 2
 
 FLOPS = 2 * ROWS * (K_IN * HID + K_IN * HID + HID * OUT)
 
@@ -189,16 +190,20 @@ def tile_multibranchfusion_t_e_kernel(
                         stop=True,
                     )
                     nc.vector.tensor_tensor(out=result[:, a, cols], in0=acc[:], in1=bias3[:, cols], op=ALU.add)
-                nc.gpsimd.tensor_scalar(
-                    out=result[:, a, :],
-                    in0=result[:, a, :],
-                    scalar1=F32_MAX,
-                    scalar2=0.0,
-                    op0=ALU.min,
-                    op1=ALU.max,
-                )
-                if a % 2 == 1:
-                    nc.sync.dma_start(out=out_rows[:, a - 1 : a + 1, :], in_=result[:, a - 1 : a + 1, :])
+                if a != VECTOR_SLAB:
+                    nc.gpsimd.tensor_scalar(
+                        out=result[:, a, :],
+                        in0=result[:, a, :],
+                        scalar1=F32_MAX,
+                        scalar2=0.0,
+                        op0=ALU.min,
+                        op1=ALU.max,
+                    )
+            nc.vector.tensor_scalar_max(
+                out=result[:, VECTOR_SLAB, :], in0=result[:, VECTOR_SLAB, :], scalar1=0.0
+            )
+            for a in range(SLABS):
+                nc.sync.dma_start(out=out_rows[:, a, :], in_=result[:, a, :])
 
         x_app = [None] * N_ROUNDS
         x_sp = [None] * N_ROUNDS

@@ -21,7 +21,6 @@ N_ROUNDS = ROWS // ROUND
 SLABS = ROUND // P
 WORDS = K_IN // 2
 F32_MAX = 3.4028234663852886e38
-VECTOR_SLAB = 2
 
 FLOPS = 2 * ROWS * (K_IN * HID + K_IN * HID + HID * OUT)
 
@@ -34,8 +33,8 @@ def tile_multibranchfusion_t_e_kernel(
         ctx.enter_context(tc.manual_schedule())
         const = ctx.enter_context(tc.tile_pool(name="const", bufs=1))
         rows_in = ctx.enter_context(tc.tile_pool(name="rows_in", bufs=1))
-        work = ctx.enter_context(tc.tile_pool(name="work", bufs=2))
-        packed = ctx.enter_context(tc.tile_pool(name="packed", bufs=3))
+        work = ctx.enter_context(tc.tile_pool(name="work", bufs=3))
+        packed = ctx.enter_context(tc.tile_pool(name="packed", bufs=4))
         rows_out = ctx.enter_context(tc.tile_pool(name="rows_out", bufs=3))
         psum = ctx.enter_context(tc.psum_pool(name="psum", bufs=8))
 
@@ -45,16 +44,20 @@ def tile_multibranchfusion_t_e_kernel(
         w2_raw_scales = const.tile([P, CARD, SUB], U8)
         nc.vector.memset(w1_raw_scales[:].bitcast(I32), 0)
         nc.vector.memset(w2_raw_scales[:].bitcast(I32), 0)
+        zero = const.tile([P, 1], F32)
+        nc.vector.memset(zero[:], 0.0)
         b12_rows = const.tile([P, P], BF16)
         nc.vector.memset(b12_rows[:], 0.0)
         b3_rows = const.tile([P, OUT], BF16)
         nc.vector.memset(b3_rows[:], 0.0)
         ones = const.tile([P, P], BF16)
         nc.vector.memset(ones[:], 1.0)
+        table_load = const.tile([P, 1], F32)
+        nc.scalar.activation(out=table_load[:], in_=zero[:], func=ACT.Relu)
 
-        def load_rows(src, r, name):
+        def load_rows(queue, src, r, name):
             rows = rows_in.tile([P, SLABS, K_IN], BF16, name="%s%d" % (name, r))
-            nc.sync.dma_start(
+            queue.dma_start(
                 out=rows[:],
                 in_=src[ROUND * r : ROUND * (r + 1), :].rearrange("(p a) k -> p a k", a=SLABS),
             )
@@ -78,24 +81,24 @@ def tile_multibranchfusion_t_e_kernel(
 
         app_rows = [None] * N_ROUNDS
         sp_rows = [None] * N_ROUNDS
-        app_rows[0] = load_rows(appearance, 0, "app")
-        sp_rows[0] = load_rows(spatial, 0, "sp")
+        def load_round(queue, r):
+            app_rows[r] = load_rows(queue, appearance, r, "app")
+            sp_rows[r] = load_rows(queue, spatial, r, "sp")
+
+        load_round(nc.sync, 0)
+        load_round(nc.gpsimd, 1)
+        nc.scalar.dma_start(out=b12_rows[0:PACK, :], in_=b1.rearrange("c (t i) -> t c i", i=RUN))
+        nc.scalar.dma_start(out=b12_rows[PACK : 2 * PACK, :], in_=b2.rearrange("c (t i) -> t c i", i=RUN))
+        nc.gpsimd.dma_start(out=b3_rows[0:CARD, :], in_=b3)
         load_scale_rows(w1_raw_scales, W1_scales)
         load_scale_rows(w2_raw_scales, W2_scales)
-        app_rows[1] = load_rows(appearance, 1, "app")
-        sp_rows[1] = load_rows(spatial, 1, "sp")
         w1_raw_words = load_words(W1_words, "w1_raw_words")
         w2_raw_words = load_words(W2_words, "w2_raw_words")
         w3_raw = const.tile([P, PACK, OUT], BF16)
         for t in range(PACK):
             nc.sync.dma_start(out=w3_raw[:, t, :], in_=W3[:, RUN * t : RUN * (t + 1), :])
         for r in range(2, N_ROUNDS):
-            app_rows[r] = load_rows(appearance, r, "app")
-            sp_rows[r] = load_rows(spatial, r, "sp")
-
-        nc.scalar.dma_start(out=b12_rows[0:PACK, :], in_=b1.rearrange("c (t i) -> t c i", i=RUN))
-        nc.scalar.dma_start(out=b12_rows[PACK : 2 * PACK, :], in_=b2.rearrange("c (t i) -> t c i", i=RUN))
-        nc.scalar.dma_start(out=b3_rows[0:CARD, :], in_=b3)
+            load_round(nc.sync, r)
 
         def side_by_side(copy, grouped, planes):
             copy(
@@ -103,7 +106,7 @@ def tile_multibranchfusion_t_e_kernel(
                 in_=planes.rearrange("p t (c i) -> p c t i", i=4),
             )
 
-        def transpose_and_quantise(rows, name):
+        def transpose(rows, name):
             grouped = work.tile([P, SLABS, P, PACK], BF16, name=name + "_grouped", align_bytes=64)
             for pair in range(SLABS // 2):
                 flipped = psum.tile([P, 2, 2, P], F32, tag="bank")
@@ -118,6 +121,9 @@ def tile_multibranchfusion_t_e_kernel(
                     out=grouped[:, 2 * pair : 2 * pair + 2, :, :].bitcast(F32),
                     in_=flipped[:].rearrange("p a u n -> p a n u"),
                 )
+            return grouped
+
+        def quantise_x(grouped, name):
             words = packed.tile([P, ROUND], I32, name=name + "_words", align_bytes=64)
             scales = packed.tile([P, ROUND], U8, name=name + "_scales", align_bytes=64)
             nc.vector.quantize_mx(
@@ -174,7 +180,6 @@ def tile_multibranchfusion_t_e_kernel(
         def output_layer(h, r):
             h_words, h_scales = h
             result = rows_out.tile([P, SLABS, OUT], F32)
-            out_rows = out[ROUND * r : ROUND * (r + 1), :].rearrange("(p a) o -> p a o", a=SLABS)
             for a in range(SLABS):
                 slab = slice(P * a, P * (a + 1))
                 for half in range(OUT // BANK):
@@ -190,27 +195,31 @@ def tile_multibranchfusion_t_e_kernel(
                         stop=True,
                     )
                     nc.vector.tensor_tensor(out=result[:, a, cols], in0=acc[:], in1=bias3[:, cols], op=ALU.add)
-                if a != VECTOR_SLAB:
-                    nc.gpsimd.tensor_scalar(
-                        out=result[:, a, :],
-                        in0=result[:, a, :],
-                        scalar1=F32_MAX,
-                        scalar2=0.0,
-                        op0=ALU.min,
-                        op1=ALU.max,
-                    )
-            nc.vector.tensor_scalar_max(
-                out=result[:, VECTOR_SLAB, :], in0=result[:, VECTOR_SLAB, :], scalar1=0.0
-            )
-            for a in range(SLABS):
-                nc.sync.dma_start(out=out_rows[:, a, :], in_=result[:, a, :])
+            return result
+
+        def relu_on_vector(x):
+            nc.vector.tensor_scalar_max(out=x, in0=x, scalar1=0.0)
+
+        def relu_on_scalar(x):
+            nc.scalar.activation(out=x, in_=x, func=ACT.Relu)
+
+        def relu_on_gpsimd(x):
+            nc.gpsimd.tensor_scalar(out=x, in0=x, scalar1=F32_MAX, scalar2=0.0, op0=ALU.min, op1=ALU.max)
+
+        def relu_and_store(relu, result, r, a, pieces=1):
+            out_rows = out[ROUND * r : ROUND * (r + 1), :].rearrange("(p a) o -> p a o", a=SLABS)
+            width = OUT // pieces
+            for piece in range(pieces):
+                cols = slice(width * piece, width * (piece + 1))
+                relu(result[:, a, cols])
+                nc.sync.dma_start(out=out_rows[:, a, cols], in_=result[:, a, cols])
 
         x_app = [None] * N_ROUNDS
         x_sp = [None] * N_ROUNDS
 
         def prepare_round(r):
-            x_app[r] = transpose_and_quantise(app_rows[r], "app")
-            x_sp[r] = transpose_and_quantise(sp_rows[r], "sp")
+            x_app[r] = quantise_x(transpose(app_rows[r], "app"), "app")
+            x_sp[r] = quantise_x(transpose(sp_rows[r], "sp"), "sp")
 
         b12_rows_f32 = const.tile([P, P], F32)
         nc.vector.tensor_copy(out=b12_rows_f32[:], in_=b12_rows[:])
@@ -226,20 +235,10 @@ def tile_multibranchfusion_t_e_kernel(
             out=bias12[:], in0=b12_cols[:, 0:PACK], in1=b12_cols[:, PACK : 2 * PACK], op=ALU.add
         )
 
-        prepare_round(1)
-
         w1 = regroup_weight_bytes(w1_raw_words, w1_raw_scales, "w1")
         w2 = regroup_weight_bytes(w2_raw_words, w2_raw_scales, "w2")
 
-        w3_grouped = const.tile([P, OUT, PACK], BF16, align_bytes=64)
-        side_by_side(nc.vector.tensor_copy, w3_grouped[:], w3_raw[:])
-        w3_words = const.tile([P, OUT], I32, align_bytes=64)
-        w3_scales = const.tile([P, OUT], U8, align_bytes=64)
-        nc.vector.quantize_mx(
-            out=w3_words[:].bitcast(FP8X4),
-            scales=w3_scales[:],
-            in_=w3_grouped[:].rearrange("p o t -> p (o t)"),
-        )
+        prepare_round(1)
 
         bias3 = const.tile([P, OUT], F32)
         for half in range(OUT // BANK):
@@ -249,12 +248,40 @@ def tile_multibranchfusion_t_e_kernel(
             nc.vector.tensor_copy(out=bias3[:, cols], in_=acc[:])
 
         h = [None] * N_ROUNDS
-        for r in range(N_ROUNDS + 1):
-            if r < N_ROUNDS:
-                h_planes = hidden_layer(x_app[r], x_sp[r])
-            if r >= 1:
-                output_layer(h[r - 1], r - 1)
-            if r < N_ROUNDS:
-                h[r] = quantise_hidden(h_planes)
-            if r + 2 < N_ROUNDS:
-                prepare_round(r + 2)
+        h_planes = hidden_layer(x_app[0], x_sp[0])
+
+        w3_grouped = const.tile([P, OUT, PACK], BF16, align_bytes=64)
+        w3_words = const.tile([P, OUT], I32, align_bytes=64)
+        w3_scales = const.tile([P, OUT], U8, align_bytes=64)
+        for half in range(OUT // BANK):
+            cols = slice(BANK * half, BANK * (half + 1))
+            side_by_side(nc.vector.tensor_copy, w3_grouped[:, cols, :], w3_raw[:, :, cols])
+            nc.vector.quantize_mx(
+                out=w3_words[:, cols].bitcast(FP8X4),
+                scales=w3_scales[:, cols],
+                in_=w3_grouped[:, cols, :].rearrange("p o t -> p (o t)"),
+            )
+
+        h[0] = quantise_hidden(h_planes)
+        prepare_round(2)
+
+        for r in range(N_ROUNDS):
+            if r + 1 < N_ROUNDS:
+                h_planes = hidden_layer(x_app[r + 1], x_sp[r + 1])
+            result = output_layer(h[r], r)
+            if r + 1 < N_ROUNDS:
+                h[r + 1] = quantise_hidden(h_planes)
+            if r + 3 < N_ROUNDS:
+                x_app[r + 3] = quantise_x(transpose(app_rows[r + 3], "app"), "app")
+                sp_grouped = transpose(sp_rows[r + 3], "sp")
+            relu_and_store(relu_on_gpsimd, result, r, 0)
+            if r + 1 < N_ROUNDS:
+                relu_and_store(relu_on_gpsimd, result, r, 1)
+                relu_and_store(relu_on_vector, result, r, 2)
+                relu_and_store(relu_on_gpsimd, result, r, 3)
+            else:
+                relu_and_store(relu_on_scalar, result, r, 1)
+                relu_and_store(relu_on_vector, result, r, 2)
+                relu_and_store(relu_on_scalar, result, r, 3, pieces=2)
+            if r + 3 < N_ROUNDS:
+                x_sp[r + 3] = quantise_x(sp_grouped, "sp")

@@ -147,7 +147,7 @@ def tile_multibranchfusion_t_e_kernel(
             return words, scales
 
         def hidden_layer(x_app, x_sp):
-            h_planes = work.tile([P, PACK, ROUND], BF16)
+            h_pairs = work.tile([P, PACK // 2, ROUND, 2], BF16)
             for t in range(PACK):
                 acc = psum.tile([P, BANK], F32, tag="bank")
                 for weight, x, first in ((w1, x_app, True), (w2, x_sp, False)):
@@ -161,13 +161,19 @@ def tile_multibranchfusion_t_e_kernel(
                         stop=not first,
                     )
                 nc.scalar.activation(
-                    out=h_planes[:, t, :], in_=acc[:], func=ACT.Relu, bias=bias12[:, t : t + 1], scale=1.0
+                    out=h_pairs[:, t // 2, :, t % 2], in_=acc[:], func=ACT.Relu, bias=bias12[:, t : t + 1], scale=1.0
                 )
-            return h_planes
+            return h_pairs
 
-        def quantise_hidden(h_planes):
+        def group_hidden(h_pairs):
             h_grouped = work.tile([P, ROUND, PACK], BF16, align_bytes=64)
-            side_by_side(nc.scalar.copy, h_grouped[:], h_planes[:])
+            nc.scalar.copy(
+                out=h_grouped[:].rearrange("p n (q e) -> p n q e", e=2),
+                in_=h_pairs[:].rearrange("p q n e -> p n q e"),
+            )
+            return h_grouped
+
+        def quantise_hidden(h_grouped):
             h_words = work.tile([P, ROUND], I32, align_bytes=64)
             h_scales = work.tile([P, ROUND], U8, align_bytes=64)
             nc.vector.quantize_mx(
@@ -177,25 +183,22 @@ def tile_multibranchfusion_t_e_kernel(
             )
             return h_words, h_scales
 
-        def output_layer(h, r):
+        def output_layer(h, result, a):
             h_words, h_scales = h
-            result = rows_out.tile([P, SLABS, OUT], F32)
-            for a in range(SLABS):
-                slab = slice(P * a, P * (a + 1))
-                for half in range(OUT // BANK):
-                    cols = slice(BANK * half, BANK * (half + 1))
-                    acc = psum.tile([P, BANK], F32, tag="bank")
-                    nc.tensor.matmul_mx(
-                        out=acc[:],
-                        lhsT=h_words[:, slab].bitcast(FP8X4),
-                        lhsT_scale=h_scales[:, slab],
-                        rhs=w3_words[:, cols].bitcast(FP8X4),
-                        rhs_scale=w3_scales[:, cols],
-                        start=True,
-                        stop=True,
-                    )
-                    nc.vector.tensor_tensor(out=result[:, a, cols], in0=acc[:], in1=bias3[:, cols], op=ALU.add)
-            return result
+            slab = slice(P * a, P * (a + 1))
+            for half in range(OUT // BANK):
+                cols = slice(BANK * half, BANK * (half + 1))
+                acc = psum.tile([P, BANK], F32, tag="bank")
+                nc.tensor.matmul_mx(
+                    out=acc[:],
+                    lhsT=h_words[:, slab].bitcast(FP8X4),
+                    lhsT_scale=h_scales[:, slab],
+                    rhs=w3_words[:, cols].bitcast(FP8X4),
+                    rhs_scale=w3_scales[:, cols],
+                    start=True,
+                    stop=True,
+                )
+                nc.vector.tensor_tensor(out=result[:, a, cols], in0=acc[:], in1=bias3[:, cols], op=ALU.add)
 
         def relu_on_vector(x):
             nc.vector.tensor_scalar_max(out=x, in0=x, scalar1=0.0)
@@ -235,10 +238,10 @@ def tile_multibranchfusion_t_e_kernel(
             out=bias12[:], in0=b12_cols[:, 0:PACK], in1=b12_cols[:, PACK : 2 * PACK], op=ALU.add
         )
 
+        app_grouped = transpose(app_rows[1], "app")
         w1 = regroup_weight_bytes(w1_raw_words, w1_raw_scales, "w1")
         w2 = regroup_weight_bytes(w2_raw_words, w2_raw_scales, "w2")
-
-        prepare_round(1)
+        sp_grouped = transpose(sp_rows[1], "sp")
 
         bias3 = const.tile([P, OUT], F32)
         for half in range(OUT // BANK):
@@ -248,7 +251,9 @@ def tile_multibranchfusion_t_e_kernel(
             nc.vector.tensor_copy(out=bias3[:, cols], in_=acc[:])
 
         h = [None] * N_ROUNDS
-        h_planes = hidden_layer(x_app[0], x_sp[0])
+        h_pairs = hidden_layer(x_app[0], x_sp[0])
+        x_app[1] = quantise_x(app_grouped, "app")
+        x_sp[1] = quantise_x(sp_grouped, "sp")
 
         w3_grouped = const.tile([P, OUT, PACK], BF16, align_bytes=64)
         w3_words = const.tile([P, OUT], I32, align_bytes=64)
@@ -262,26 +267,36 @@ def tile_multibranchfusion_t_e_kernel(
                 in_=w3_grouped[:, cols, :].rearrange("p o t -> p (o t)"),
             )
 
-        h[0] = quantise_hidden(h_planes)
+        h[0] = quantise_hidden(group_hidden(h_pairs))
         prepare_round(2)
 
         for r in range(N_ROUNDS):
-            if r + 1 < N_ROUNDS:
-                h_planes = hidden_layer(x_app[r + 1], x_sp[r + 1])
-            result = output_layer(h[r], r)
-            if r + 1 < N_ROUNDS:
-                h[r + 1] = quantise_hidden(h_planes)
-            if r + 3 < N_ROUNDS:
-                x_app[r + 3] = quantise_x(transpose(app_rows[r + 3], "app"), "app")
+            hidden_ahead = r + 1 < N_ROUNDS
+            rows_ahead = r + 3 < N_ROUNDS
+            if hidden_ahead:
+                h_pairs = hidden_layer(x_app[r + 1], x_sp[r + 1])
+            result = rows_out.tile([P, SLABS, OUT], F32, name="result")
+            output_layer(h[r], result, 0)
+            if rows_ahead:
+                app_grouped = transpose(app_rows[r + 3], "app")
+            if hidden_ahead:
+                h_grouped = group_hidden(h_pairs)
+            for a in range(1, SLABS):
+                output_layer(h[r], result, a)
+            if hidden_ahead:
+                h[r + 1] = quantise_hidden(h_grouped)
+            if rows_ahead:
                 sp_grouped = transpose(sp_rows[r + 3], "sp")
-            relu_and_store(relu_on_gpsimd, result, r, 0)
-            if r + 1 < N_ROUNDS:
+                x_app[r + 3] = quantise_x(app_grouped, "app")
+            if hidden_ahead:
+                relu_and_store(relu_on_gpsimd, result, r, 0)
                 relu_and_store(relu_on_gpsimd, result, r, 1)
                 relu_and_store(relu_on_vector, result, r, 2)
                 relu_and_store(relu_on_gpsimd, result, r, 3)
             else:
+                relu_and_store(relu_on_scalar, result, r, 0)
                 relu_and_store(relu_on_scalar, result, r, 1)
                 relu_and_store(relu_on_vector, result, r, 2)
                 relu_and_store(relu_on_scalar, result, r, 3, pieces=2)
-            if r + 3 < N_ROUNDS:
+            if rows_ahead:
                 x_sp[r + 3] = quantise_x(sp_grouped, "sp")

@@ -147,7 +147,7 @@ def tile_multibranchfusion_t_e_kernel(
             return words, scales
 
         def hidden_layer(x_app, x_sp):
-            h_pairs = work.tile([P, PACK // 2, ROUND, 2], BF16)
+            h_planes = work.tile([P, PACK, ROUND], BF16)
             for t in range(PACK):
                 acc = psum.tile([P, BANK], F32, tag="bank")
                 for weight, x, first in ((w1, x_app, True), (w2, x_sp, False)):
@@ -161,16 +161,13 @@ def tile_multibranchfusion_t_e_kernel(
                         stop=not first,
                     )
                 nc.scalar.activation(
-                    out=h_pairs[:, t // 2, :, t % 2], in_=acc[:], func=ACT.Relu, bias=bias12[:, t : t + 1], scale=1.0
+                    out=h_planes[:, t, :], in_=acc[:], func=ACT.Relu, bias=bias12[:, t : t + 1], scale=1.0
                 )
-            return h_pairs
+            return h_planes
 
-        def group_hidden(h_pairs):
+        def group_hidden(h_planes):
             h_grouped = work.tile([P, ROUND, PACK], BF16, align_bytes=64)
-            nc.scalar.copy(
-                out=h_grouped[:].rearrange("p n (q e) -> p n q e", e=2),
-                in_=h_pairs[:].rearrange("p q n e -> p n q e"),
-            )
+            side_by_side(nc.scalar.copy, h_grouped[:], h_planes[:])
             return h_grouped
 
         def quantise_hidden(h_grouped):
@@ -251,7 +248,7 @@ def tile_multibranchfusion_t_e_kernel(
             nc.vector.tensor_copy(out=bias3[:, cols], in_=acc[:])
 
         h = [None] * N_ROUNDS
-        h_pairs = hidden_layer(x_app[0], x_sp[0])
+        h_planes = hidden_layer(x_app[0], x_sp[0])
         x_app[1] = quantise_x(app_grouped, "app")
         x_sp[1] = quantise_x(sp_grouped, "sp")
 
@@ -267,20 +264,20 @@ def tile_multibranchfusion_t_e_kernel(
                 in_=w3_grouped[:, cols, :].rearrange("p o t -> p (o t)"),
             )
 
-        h[0] = quantise_hidden(group_hidden(h_pairs))
+        h[0] = quantise_hidden(group_hidden(h_planes))
         prepare_round(2)
 
         for r in range(N_ROUNDS):
             hidden_ahead = r + 1 < N_ROUNDS
             rows_ahead = r + 3 < N_ROUNDS
             if hidden_ahead:
-                h_pairs = hidden_layer(x_app[r + 1], x_sp[r + 1])
+                h_planes = hidden_layer(x_app[r + 1], x_sp[r + 1])
             result = rows_out.tile([P, SLABS, OUT], F32, name="result")
             output_layer(h[r], result, 0)
             if rows_ahead:
                 app_grouped = transpose(app_rows[r + 3], "app")
             if hidden_ahead:
-                h_grouped = group_hidden(h_pairs)
+                h_grouped = group_hidden(h_planes)
             for a in range(1, SLABS):
                 output_layer(h[r], result, a)
             if hidden_ahead:
@@ -294,9 +291,7 @@ def tile_multibranchfusion_t_e_kernel(
                 relu_and_store(relu_on_vector, result, r, 2)
                 relu_and_store(relu_on_gpsimd, result, r, 3)
             else:
-                relu_and_store(relu_on_scalar, result, r, 0)
-                relu_and_store(relu_on_scalar, result, r, 1)
-                relu_and_store(relu_on_vector, result, r, 2)
-                relu_and_store(relu_on_scalar, result, r, 3, pieces=2)
+                for a in range(SLABS):
+                    relu_and_store(relu_on_scalar, result, r, a, pieces=2 if a == SLABS - 1 else 1)
             if rows_ahead:
                 x_sp[r + 3] = quantise_x(sp_grouped, "sp")

@@ -20,6 +20,7 @@ ROUND = 512
 N_ROUNDS = ROWS // ROUND
 SLABS = ROUND // P
 WORDS = K_IN // 2
+WARM_UP = 4
 F32_MAX = 3.4028234663852886e38
 
 FLOPS = 2 * ROWS * (K_IN * HID + K_IN * HID + HID * OUT)
@@ -48,10 +49,10 @@ def tile_multibranchfusion_t_e_kernel(
         nc.vector.memset(zero[:], 0.0)
         b12_rows = const.tile([P, P], BF16)
         nc.vector.memset(b12_rows[:], 0.0)
+        ones = const.tile([P, BANK], BF16)
+        nc.vector.memset(ones[:], 1.0)
         b3_rows = const.tile([P, OUT], BF16)
         nc.vector.memset(b3_rows[:], 0.0)
-        ones = const.tile([P, P], BF16)
-        nc.vector.memset(ones[:], 1.0)
         table_load = const.tile([P, 1], F32)
         nc.scalar.activation(out=table_load[:], in_=zero[:], func=ACT.Relu)
 
@@ -224,6 +225,10 @@ def tile_multibranchfusion_t_e_kernel(
         b12_rows_f32 = const.tile([P, P], F32)
         nc.vector.tensor_copy(out=b12_rows_f32[:], in_=b12_rows[:])
 
+        warm_up = psum.tile([P, BANK], F32, tag="bank")
+        for k in range(WARM_UP):
+            nc.tensor.matmul(out=warm_up[:], lhsT=ones[:, 0:P], rhs=ones[:], start=True, stop=True)
+
         prepare_round(0)
 
         b12_flipped = psum.tile([P, BANK], F32, tag="bank")
@@ -244,7 +249,7 @@ def tile_multibranchfusion_t_e_kernel(
         for half in range(OUT // BANK):
             cols = slice(BANK * half, BANK * (half + 1))
             acc = psum.tile([P, BANK], F32, tag="bank")
-            nc.tensor.matmul(out=acc[:], lhsT=ones[:], rhs=b3_rows[:, cols], start=True, stop=True)
+            nc.tensor.matmul(out=acc[:], lhsT=ones[:, 0:P], rhs=b3_rows[:, cols], start=True, stop=True)
             nc.vector.tensor_copy(out=bias3[:, cols], in_=acc[:])
 
         h = [None] * N_ROUNDS
@@ -291,7 +296,8 @@ def tile_multibranchfusion_t_e_kernel(
                 relu_and_store(relu_on_vector, result, r, 2)
                 relu_and_store(relu_on_gpsimd, result, r, 3)
             else:
-                for a in range(SLABS):
-                    relu_and_store(relu_on_scalar, result, r, a, pieces=2 if a == SLABS - 1 else 1)
+                for a in range(SLABS - 1):
+                    relu_and_store(relu_on_scalar, result, r, a, pieces=2)
+                relu_and_store(relu_on_vector, result, r, SLABS - 1, pieces=2)
             if rows_ahead:
                 x_sp[r + 3] = quantise_x(sp_grouped, "sp")

import concourse.mybir as mybir
from concourse.masks import make_identity
from contextlib import ExitStack

F32 = mybir.dt.float32
BF16 = mybir.dt.bfloat16
I32 = mybir.dt.int32
U8 = mybir.dt.uint8
FP8X4 = mybir.dt.float8_e4m3fn_x4
ALU = mybir.AluOpType
ACT = mybir.ActivationFunctionType

P = 128
PACK = 4
BANK = 512
ROWS, K_IN, HID, OUT = 4096, 512, 512, 1024
CARD, SUB = 16, 32
RUN = SUB // PACK
ROUND = 512
N_ROUNDS = ROWS // ROUND
SLABS = ROUND // P
WORDS = K_IN // 2
WARM_UP = 4
F32_MAX = 3.4028234663852886e38

FLOPS = 2 * ROWS * (K_IN * HID + K_IN * HID + HID * OUT)


def tile_multibranchfusion_t_e_kernel(
    tc, appearance, spatial, W1_words, W1_scales, b1, W2_words, W2_scales, b2, W3, b3, out
):
    nc = tc.nc
    with ExitStack() as ctx:
        ctx.enter_context(tc.manual_schedule())
        const = ctx.enter_context(tc.tile_pool(name="const", bufs=1))
        rows_in = ctx.enter_context(tc.tile_pool(name="rows_in", bufs=1))
        work = ctx.enter_context(tc.tile_pool(name="work", bufs=3))
        packed = ctx.enter_context(tc.tile_pool(name="packed", bufs=4))
        rows_out = ctx.enter_context(tc.tile_pool(name="rows_out", bufs=3))
        psum = ctx.enter_context(tc.psum_pool(name="psum", bufs=8))

        identity = const.tile([P, P], F32)
        make_identity(nc, identity[:])
        w1_raw_scales = const.tile([P, CARD, SUB], U8)
        w2_raw_scales = const.tile([P, CARD, SUB], U8)
        nc.vector.memset(w1_raw_scales[:].bitcast(I32), 0)
        nc.vector.memset(w2_raw_scales[:].bitcast(I32), 0)
        zero = const.tile([P, 1], F32)
        nc.vector.memset(zero[:], 0.0)
        b12_rows = const.tile([P, P], BF16)
        nc.vector.memset(b12_rows[:], 0.0)
        ones = const.tile([P, BANK], BF16)
        nc.vector.memset(ones[:], 1.0)
        b3_rows = const.tile([P, OUT], BF16)
        nc.vector.memset(b3_rows[:], 0.0)
        table_load = const.tile([P, 1], F32)
        nc.scalar.activation(out=table_load[:], in_=zero[:], func=ACT.Relu)

        def load_rows(queue, src, r, name):
            rows = rows_in.tile([P, SLABS, K_IN], BF16, name="%s%d" % (name, r))
            queue.dma_start(
                out=rows[:],
                in_=src[ROUND * r : ROUND * (r + 1), :].rearrange("(p a) k -> p a k", a=SLABS),
            )
            return rows

        def load_scale_rows(raw_scales, scales_dram):
            for quadrant in range(4):
                nc.sync.dma_start(
                    out=raw_scales[32 * quadrant : 32 * quadrant + 4].bitcast(I32),
                    in_=scales_dram.bitcast(I32)[:, 4 * quadrant : 4 * quadrant + 4, :].rearrange(
                        "c q s -> q c s"
                    ),
                )

        def load_words(words_dram, name):
            raw_words = const.tile([P, CARD, SUB], I32, name=name)
            nc.sync.dma_start(
                out=raw_words[:], in_=words_dram.rearrange("c p s t -> p c (s t)").bitcast(I32)
            )
            return raw_words

        app_rows = [None] * N_ROUNDS
        sp_rows = [None] * N_ROUNDS
        def load_round(queue, r):
            app_rows[r] = load_rows(queue, appearance, r, "app")
            sp_rows[r] = load_rows(queue, spatial, r, "sp")

        load_round(nc.sync, 0)
        load_round(nc.gpsimd, 1)
        nc.scalar.dma_start(out=b12_rows[0:PACK, :], in_=b1.rearrange("c (t i) -> t c i", i=RUN))
        nc.scalar.dma_start(out=b12_rows[PACK : 2 * PACK, :], in_=b2.rearrange("c (t i) -> t c i", i=RUN))
        nc.gpsimd.dma_start(out=b3_rows[0:CARD, :], in_=b3)
        load_scale_rows(w1_raw_scales, W1_scales)
        load_scale_rows(w2_raw_scales, W2_scales)
        w1_raw_words = load_words(W1_words, "w1_raw_words")
        w2_raw_words = load_words(W2_words, "w2_raw_words")
        w3_raw = const.tile([P, PACK, OUT], BF16)
        for t in range(PACK):
            nc.sync.dma_start(out=w3_raw[:, t, :], in_=W3[:, RUN * t : RUN * (t + 1), :])
        for r in range(2, N_ROUNDS):
            load_round(nc.sync, r)

        def side_by_side(copy, grouped, planes):
            copy(
                out=grouped.rearrange("p (c i) t -> p c t i", i=4),
                in_=planes.rearrange("p t (c i) -> p c t i", i=4),
            )

        def transpose(rows, name):
            grouped = work.tile([P, SLABS, P, PACK], BF16, name=name + "_grouped", align_bytes=64)
            for pair in range(SLABS // 2):
                flipped = psum.tile([P, 2, 2, P], F32, tag="bank")
                for a in range(2):
                    for u in range(2):
                        nc.tensor.transpose(
                            out=flipped[:, a, u, :],
                            in_=rows[:, 2 * pair + a, :].bitcast(F32)[:, u:WORDS:2],
                            identity=identity[:],
                        )
                nc.scalar.copy(
                    out=grouped[:, 2 * pair : 2 * pair + 2, :, :].bitcast(F32),
                    in_=flipped[:].rearrange("p a u n -> p a n u"),
                )
            return grouped

        def quantise_x(grouped, name):
            words = packed.tile([P, ROUND], I32, name=name + "_words", align_bytes=64)
            scales = packed.tile([P, ROUND], U8, name=name + "_scales", align_bytes=64)
            nc.vector.quantize_mx(
                out=words[:].bitcast(FP8X4),
                scales=scales[:],
                in_=grouped[:].rearrange("p a n t -> p (a n t)"),
            )
            return words, scales

        def regroup_weight_bytes(raw_words, raw_scales, name):
            words = const.tile([P, PACK, P], I32, name=name + "_words", align_bytes=64)
            scales = const.tile([P, PACK, P], U8, name=name + "_scales", align_bytes=64)
            nc.vector.tensor_copy(
                out=words[:].rearrange("p t (c i) -> p t c i", i=RUN),
                in_=raw_words[:].rearrange("p c (t i) -> p t c i", i=RUN),
            )
            nc.vector.tensor_copy(
                out=scales[:].bitcast(I32).rearrange("p t (c w) -> p t c w", w=RUN // 4),
                in_=raw_scales[:].bitcast(I32).rearrange("p c (t w) -> p t c w", w=RUN // 4),
            )
            return words, scales

        def hidden_layer(x_app, x_sp):
            h_planes = work.tile([P, PACK, ROUND], BF16)
            for t in range(PACK):
                acc = psum.tile([P, BANK], F32, tag="bank")
                for weight, x, first in ((w1, x_app, True), (w2, x_sp, False)):
                    nc.tensor.matmul_mx(
                        out=acc[:],
                        lhsT=weight[0][:, t, :].bitcast(FP8X4),
                        lhsT_scale=weight[1][:, t, :],
                        rhs=x[0][:].bitcast(FP8X4),
                        rhs_scale=x[1][:],
                        start=first,
                        stop=not first,
                    )
                nc.scalar.activation(
                    out=h_planes[:, t, :], in_=acc[:], func=ACT.Relu, bias=bias12[:, t : t + 1], scale=1.0
                )
            return h_planes

        def group_hidden(h_planes):
            h_grouped = work.tile([P, ROUND, PACK], BF16, align_bytes=64)
            side_by_side(nc.scalar.copy, h_grouped[:], h_planes[:])
            return h_grouped

        def quantise_hidden(h_grouped):
            h_words = work.tile([P, ROUND], I32, align_bytes=64)
            h_scales = work.tile([P, ROUND], U8, align_bytes=64)
            nc.vector.quantize_mx(
                out=h_words[:].bitcast(FP8X4),
                scales=h_scales[:],
                in_=h_grouped[:].rearrange("p n t -> p (n t)"),
            )
            return h_words, h_scales

        def output_layer(h, result, a):
            h_words, h_scales = h
            slab = slice(P * a, P * (a + 1))
            for half in range(OUT // BANK):
                cols = slice(BANK * half, BANK * (half + 1))
                acc = psum.tile([P, BANK], F32, tag="bank")
                nc.tensor.matmul_mx(
                    out=acc[:],
                    lhsT=h_words[:, slab].bitcast(FP8X4),
                    lhsT_scale=h_scales[:, slab],
                    rhs=w3_words[:, cols].bitcast(FP8X4),
                    rhs_scale=w3_scales[:, cols],
                    start=True,
                    stop=True,
                )
                nc.vector.tensor_tensor(out=result[:, a, cols], in0=acc[:], in1=bias3[:, cols], op=ALU.add)

        def relu_on_vector(x):
            nc.vector.tensor_scalar_max(out=x, in0=x, scalar1=0.0)

        def relu_on_scalar(x):
            nc.scalar.activation(out=x, in_=x, func=ACT.Relu)

        def relu_on_gpsimd(x):
            nc.gpsimd.tensor_scalar(out=x, in0=x, scalar1=F32_MAX, scalar2=0.0, op0=ALU.min, op1=ALU.max)

        def relu_and_store(relu, result, r, a, pieces=1):
            out_rows = out[ROUND * r : ROUND * (r + 1), :].rearrange("(p a) o -> p a o", a=SLABS)
            width = OUT // pieces
            for piece in range(pieces):
                cols = slice(width * piece, width * (piece + 1))
                relu(result[:, a, cols])
                nc.sync.dma_start(out=out_rows[:, a, cols], in_=result[:, a, cols])

        x_app = [None] * N_ROUNDS
        x_sp = [None] * N_ROUNDS

        def prepare_round(r):
            x_app[r] = quantise_x(transpose(app_rows[r], "app"), "app")
            x_sp[r] = quantise_x(transpose(sp_rows[r], "sp"), "sp")

        b12_rows_f32 = const.tile([P, P], F32)
        nc.vector.tensor_copy(out=b12_rows_f32[:], in_=b12_rows[:])

        warm_up = psum.tile([P, BANK], F32, tag="bank")
        for k in range(WARM_UP):
            nc.tensor.matmul(out=warm_up[:], lhsT=ones[:, 0:P], rhs=ones[:], start=True, stop=True)

        prepare_round(0)

        b12_flipped = psum.tile([P, BANK], F32, tag="bank")
        nc.tensor.transpose(out=b12_flipped[:, 0:P], in_=b12_rows_f32[:], identity=identity[:])
        b12_cols = const.tile([P, 2 * PACK], F32)
        nc.vector.tensor_copy(out=b12_cols[:], in_=b12_flipped[:, 0 : 2 * PACK])
        bias12 = const.tile([P, PACK], F32)
        nc.vector.tensor_tensor(
            out=bias12[:], in0=b12_cols[:, 0:PACK], in1=b12_cols[:, PACK : 2 * PACK], op=ALU.add
        )

        app_grouped = transpose(app_rows[1], "app")
        w1 = regroup_weight_bytes(w1_raw_words, w1_raw_scales, "w1")
        w2 = regroup_weight_bytes(w2_raw_words, w2_raw_scales, "w2")
        sp_grouped = transpose(sp_rows[1], "sp")

        bias3 = const.tile([P, OUT], F32)
        for half in range(OUT // BANK):
            cols = slice(BANK * half, BANK * (half + 1))
            acc = psum.tile([P, BANK], F32, tag="bank")
            nc.tensor.matmul(out=acc[:], lhsT=ones[:, 0:P], rhs=b3_rows[:, cols], start=True, stop=True)
            nc.vector.tensor_copy(out=bias3[:, cols], in_=acc[:])

        h = [None] * N_ROUNDS
        h_planes = hidden_layer(x_app[0], x_sp[0])
        x_app[1] = quantise_x(app_grouped, "app")
        x_sp[1] = quantise_x(sp_grouped, "sp")

        w3_grouped = const.tile([P, OUT, PACK], BF16, align_bytes=64)
        w3_words = const.tile([P, OUT], I32, align_bytes=64)
        w3_scales = const.tile([P, OUT], U8, align_bytes=64)
        for half in range(OUT // BANK):
            cols = slice(BANK * half, BANK * (half + 1))
            side_by_side(nc.vector.tensor_copy, w3_grouped[:, cols, :], w3_raw[:, :, cols])
            nc.vector.quantize_mx(
                out=w3_words[:, cols].bitcast(FP8X4),
                scales=w3_scales[:, cols],
                in_=w3_grouped[:, cols, :].rearrange("p o t -> p (o t)"),
            )

        h[0] = quantise_hidden(group_hidden(h_planes))
        prepare_round(2)

        for r in range(N_ROUNDS):
            hidden_ahead = r + 1 < N_ROUNDS
            rows_ahead = r + 3 < N_ROUNDS
            if hidden_ahead:
                h_planes = hidden_layer(x_app[r + 1], x_sp[r + 1])
            result = rows_out.tile([P, SLABS, OUT], F32, name="result")
            output_layer(h[r], result, 0)
            if rows_ahead:
                app_grouped = transpose(app_rows[r + 3], "app")
            if hidden_ahead:
                h_grouped = group_hidden(h_planes)
            for a in range(1, SLABS):
                output_layer(h[r], result, a)
            if hidden_ahead:
                h[r + 1] = quantise_hidden(h_grouped)
            if rows_ahead:
                sp_grouped = transpose(sp_rows[r + 3], "sp")
                x_app[r + 3] = quantise_x(app_grouped, "app")
            if hidden_ahead:
                relu_and_store(relu_on_gpsimd, result, r, 0)
                relu_and_store(relu_on_gpsimd, result, r, 1)
                relu_and_store(relu_on_vector, result, r, 2)
                relu_and_store(relu_on_gpsimd, result, r, 3)
            else:
                for a in range(SLABS - 1):
                    relu_and_store(relu_on_scalar, result, r, a, pieces=2)
                relu_and_store(relu_on_vector, result, r, SLABS - 1, pieces=2)
            if rows_ahead:
                x_sp[r + 3] = quantise_x(sp_grouped, "sp")
